import numpy as np
import ml_dtypes


def mxq(x, axis, fmt="e4m3"):
    dtype, down = {"e4m3": (ml_dtypes.float8_e4m3fn, 7), "e5m2": (ml_dtypes.float8_e5m2, 14)}[fmt]
    v = np.moveaxis(np.asarray(x, np.float32).astype(ml_dtypes.bfloat16).astype(np.float64), axis, -1)
    blocks = v.reshape(v.shape[:-1] + (-1, 32))
    amax = np.abs(blocks).max(-1, keepdims=True)
    byte = np.maximum(np.where(amax > 0, np.frexp(amax)[1] - 1 + 127, 0) - down, 1)
    scale = np.exp2(byte - 127.0)
    codes = (blocks / scale).astype(np.float32).astype(dtype).astype(np.float64)
    return np.moveaxis((codes * scale).reshape(v.shape), -1, axis)


WIDE = False


def mx_kscale(k):
    if not WIDE:
        return np.ones(k)
    levels = np.array([10, -10, 5, -5, 0])
    if k % 512:
        return np.exp2(np.random.permutation(np.resize(levels, k // 32))).repeat(32)
    a = np.empty((k // 512, 16))
    for p in range(k // 512):
        a[p, :8] = np.random.permutation(np.resize(levels, 8))
        for g in range(8):
            far = levels[np.abs(levels - a[p, g]) >= 10]
            a[p, g + 8] = far[np.random.randint(len(far))]
    return np.exp2(a.ravel()).repeat(32)


BF16 = ml_dtypes.bfloat16


def bf(x):
    return np.asarray(x, np.float32).astype(BF16)


def f64(x):
    return np.asarray(x).astype(np.float64)


E2M1 = np.array([0.0, 0.5, 1.0, 1.5, 2.0, 3.0, 4.0, 6.0, -0.0, -0.5, -1.0, -1.5, -2.0, -3.0, -4.0, -6.0])


def pack_weight(w, fmt):
    k, n = w.shape
    w = f64(bf(w)).reshape(k // 32, 32, n)
    amax = np.abs(w).max(1)
    if fmt == "e4m3":
        byte = np.frexp(amax)[1] - 1 + 127 - 7
    else:
        mant, ex = np.frexp(amax / 6.0)
        byte = np.where(mant > 0.5, ex, ex - 1) + 127
    byte = np.clip(np.where(amax > 0, byte, 1), 1, 254)
    scaled = (w * np.exp2(127.0 - byte)[:, None, :]).reshape(k, n).astype(np.float32)
    by_word = np.ascontiguousarray(scaled.reshape(k // 512, 128, 4, n).transpose(0, 1, 3, 2))
    if fmt == "e4m3":
        words = by_word.astype(ml_dtypes.float8_e4m3fn).view(np.uint8)
    else:
        c = by_word.astype(ml_dtypes.float4_e2m1fn).view(np.uint8) & 0xF
        words = c[..., 0::2] | (c[..., 1::2] << 4)
    return np.ascontiguousarray(words), np.ascontiguousarray(byte.astype(np.uint8).reshape(k // 512, 16, n))


def unpack_weight(words, scales, fmt):
    g, p, n, _ = words.shape
    if fmt == "e4m3":
        vals = np.ascontiguousarray(words).view(ml_dtypes.float8_e4m3fn).astype(np.float64)
    else:
        nib = np.empty((g, p, n, 4), np.uint8)
        nib[..., 0::2] = words & 0xF
        nib[..., 1::2] = words >> 4
        vals = E2M1[nib]
    vals = vals * np.repeat(np.exp2(scales.astype(np.float64) - 127.0), 8, axis=1)[..., None]
    return vals.transpose(0, 1, 3, 2).reshape(g * 512, n)
def pack4(w):
    words, scales = pack_weight(w, "e2m1")
    return words.reshape(words.shape[0], 128, -1), scales


def unpack4(words, scales):
    return unpack_weight(words.reshape(words.shape[0], 128, -1, 2), scales, "e2m1")


N, F, H = 1536, 512, 512
SIG = 1.5


def draw_adj():
    r = np.random.uniform(0.5, 1.5, (N, 1))
    return 2.0 * r * np.exp(SIG * np.random.standard_normal((N, N)) - 0.5 * SIG * SIG) / N


def draw0():
    s, t = mx_kscale(F), mx_kscale(N)
    x_init = bf(np.random.standard_normal((N, F)) * s / t[:, None])
    adj1 = bf(draw_adj() * t)
    words, scales = pack4(np.random.standard_normal((F, H)) * 4.0 / np.sqrt(F) / s[:, None])
    return {"x_init": x_init,
            "adj1": adj1,
            "W1_words": words,
            "W1_scales": scales,
            "b1": bf(np.random.standard_normal(H) * 0.3)}


def core(x_init, adj1, W1_words, W1_scales, b1):
    support = mxq(f64(x_init), 1, "e4m3") @ unpack4(W1_words, W1_scales)
    y = (mxq(f64(adj1), 1, "e4m3") @ mxq(support, 0, "e4m3")) + f64(b1)
    return np.maximum(y, 0.0)


def e4m3fn_bytes(y):
    return np.clip(np.asarray(y, np.float64), -448.0, 448.0).astype(np.float32).astype(ml_dtypes.float8_e4m3fn).view(np.uint8)


def e4m3fn_values(b):
    return np.asarray(b, np.uint8).view(ml_dtypes.float8_e4m3fn).astype(np.float64)


def setup_inputs():
    d = draw0()
    x0 = np.asarray(d['adj1']).astype(np.float64)
    s = (np.max(np.abs(x0), axis=(0,), keepdims=True) / 448.0).astype(np.float32)
    out = {}
    for k, v in d.items():
        if k == 'adj1':
            out['adj1_bytes'] = e4m3fn_bytes(x0 / s.astype(np.float64))
            out['adj1_scale'] = s
        else:
            out[k] = v
    return out


def reference(x_init, adj1_bytes, adj1_scale, W1_words, W1_scales, b1):
    return core(x_init, e4m3fn_values(adj1_bytes) * adj1_scale.astype(np.float64), W1_words, W1_scales, b1)

@@ -1,0 +1,273 @@
+from contextlib import ExitStack
+
+import concourse.mybir as mybir
+from concourse.masks import make_identity
+
+NODES, FEAT, HID = 1536, 512, 512
+
+F32 = mybir.dt.float32
+BF16 = mybir.dt.bfloat16
+I32 = mybir.dt.int32
+U32 = mybir.dt.uint32
+U8 = mybir.dt.uint8
+E4M3 = mybir.dt.float8_e4m3fn
+E4M3X4 = mybir.dt.float8_e4m3fn_x4
+E2M1X4 = mybir.dt.float4_e2m1fn_x4
+ALU = mybir.AluOpType
+ACT = mybir.ActivationFunctionType
+
+P = 128
+K_PASS = 512
+PASSES = NODES // K_PASS
+PAIRS = NODES // (2 * P)
+
+FLOPS = 2 * NODES * FEAT * HID + 2 * NODES * NODES * HID
+
+
+def tile_gcn_pa_w4_kernel(tc, x_init, adj_bytes, adj_scale, w_words, w_scales, b1, out):
+    nc = tc.nc
+    with ExitStack() as ctx:
+        keep = ctx.enter_context(tc.tile_pool(name="keep", bufs=1))
+        raw = ctx.enter_context(tc.tile_pool(name="raw", bufs=6))
+        xraw = ctx.enter_context(tc.tile_pool(name="xraw", bufs=3))
+        grp = ctx.enter_context(tc.tile_pool(name="grp", bufs=3))
+        agrp = ctx.enter_context(tc.tile_pool(name="agrp", bufs=6))
+        outs = ctx.enter_context(tc.tile_pool(name="outs", bufs=4))
+        tp = ctx.enter_context(tc.psum_pool(name="tp", bufs=5))
+        ps2 = ctx.enter_context(tc.psum_pool(name="ps2", bufs=3))
+
+        ident = keep.tile([P, P], F32, name="ident")
+        make_identity(nc, ident[:])
+
+        scale = keep.tile([P, NODES], F32, name="scale")
+        bias = keep.tile([P, HID], BF16, name="bias")
+        w_codes = keep.tile([P, 2 * HID], U8, name="w_codes", align_bytes=64)
+        w_plane = keep.tile([P, HID], U8, name="w_plane", align_bytes=64)
+        x_codes = keep.tile([P, PASSES, K_PASS], U32, name="x_codes", align_bytes=64)
+        x_plane = keep.tile([P, PASSES, K_PASS], U8, name="x_plane", align_bytes=64)
+        s_codes = keep.tile([P, PASSES, HID], U32, name="s_codes", align_bytes=64)
+        s_plane = keep.tile([P, PASSES, HID], U8, name="s_plane", align_bytes=64)
+        a_codes = keep.tile([P, PAIRS, PASSES, 2 * P], U32, name="a_codes", align_bytes=64)
+        a_plane = keep.tile([P, PAIRS, PASSES, 2 * P], U8, name="a_plane", align_bytes=64)
+        a_vals = keep.tile([P, PAIRS, 2, NODES], BF16, name="a_vals")
+
+        a_raw = {}
+        x_raw = {}
+
+        def load_adj(q, c=0, pieces=1):
+            if c == 0:
+                t = raw.tile([P, 2, NODES], U8, name="a_raw_t")
+                a_raw[q] = t
+            w = NODES // pieces
+            cols = slice(w * c, w * (c + 1))
+            nc.sync.dma_start(
+                out=a_raw[q][:, :, cols],
+                in_=adj_bytes[2 * P * q : 2 * P * (q + 1), cols].rearrange("(m j) k -> m j k", j=2),
+            )
+
+        def load_x(g):
+            t = xraw.tile([P, 4, FEAT], BF16, name="x_raw_t")
+            nc.sync.dma_start(
+                out=t[:], in_=x_init[K_PASS * g : K_PASS * (g + 1), :].rearrange("(m t) f -> m t f", t=4)
+            )
+            x_raw[g] = t
+
+        def load_scale(g):
+            cols = slice(K_PASS * g, K_PASS * (g + 1))
+            nc.sync.dma_start(
+                out=scale[:, cols], in_=adj_scale[:, cols].rearrange("o k -> (o k)").partition_broadcast(P)
+            )
+
+        def load_w():
+            nc.sync.dma_start(out=w_codes[:].bitcast(I32), in_=w_words[0].bitcast(I32))
+            for q in range(4):
+                nc.sync.dma_start(
+                    out=w_plane[32 * q : 32 * q + 4, :].bitcast(I32),
+                    in_=w_scales[0, 4 * q : 4 * q + 4, :].bitcast(I32),
+                )
+
+        def adj_mult(i, c=0, pieces=1):
+            q, j = divmod(i, 2)
+            w = NODES // pieces
+            cols = slice(w * c, w * (c + 1))
+            nc.vector.tensor_tensor(
+                out=a_vals[:, q, j, cols],
+                in0=a_raw[q][:, j, cols].bitcast(E4M3),
+                in1=scale[:, cols],
+                op=ALU.mult,
+            )
+
+        def turn(src_words, dst):
+            bank = tp.tile([P, 4, P], F32, name="bank")
+            for a in range(2):
+                for u in range(2):
+                    nc.tensor.transpose(bank[:, 2 * a + u, :], src_words(a, u), ident[:])
+            nc.scalar.copy(
+                out=dst.bitcast(F32).rearrange("p (a m u) -> p a m u", a=2, u=2),
+                in_=bank[:].rearrange("p (a u) m -> p a m u", a=2),
+            )
+
+        x_grp = {}
+
+        def x_turn(g):
+            t = grp.tile([P, 4 * K_PASS], BF16, name="x_grp_t", align_bytes=64)
+            x_grp[g] = t
+            words = x_raw[g][:].rearrange("p t f -> p (t f)").bitcast(F32)
+            for b in range(2):
+                turn(
+                    lambda a, u: words[:, 256 * (2 * b + a) + u : 256 * (2 * b + a + 1) : 2],
+                    t[:, 1024 * b : 1024 * (b + 1)],
+                )
+
+        def x_quant(g):
+            nc.vector.quantize_mx(out=x_codes[:, g, :].bitcast(E4M3X4), scales=x_plane[:, g, :], in_=x_grp[g][:])
+
+        s_grp = {}
+
+        def stage1(g):
+            t = grp.tile([P, 4 * HID], BF16, name="s_grp_t", align_bytes=64)
+            s_grp[g] = t
+            for c in range(4):
+                bank = tp.tile([P, 4, P], F32, name="bank")
+                for k in range(4):
+                    cols = slice(P * k, P * (k + 1))
+                    nc.tensor.matmul_mx(
+                        out=bank[:, k, :],
+                        lhsT=x_codes[:, g, cols].bitcast(E4M3X4),
+                        lhsT_scale=x_plane[:, g, cols],
+                        rhs=w_codes[:, 256 * c : 256 * (c + 1)].bitcast(E2M1X4),
+                        rhs_scale=w_plane[:, P * c : P * (c + 1)],
+                        start=True,
+                        stop=True,
+                    )
+                nc.scalar.copy(
+                    out=t[:, 512 * c : 512 * (c + 1)].rearrange("p (n t) -> p n t", t=4),
+                    in_=bank[:].rearrange("p t n -> p n t"),
+                )
+
+        def s_quant(g):
+            nc.vector.quantize_mx(out=s_codes[:, g, :].bitcast(E4M3X4), scales=s_plane[:, g, :], in_=s_grp[g][:])
+
+        a_grp = {}
+
+        def adj_turn(q, passes=range(PASSES)):
+            for g in passes:
+                t = agrp.tile([P, 8 * P], BF16, name="a_grp_t", align_bytes=64)
+                a_grp[q, g] = t
+                turn(
+                    lambda a, u: a_vals[:, q, a, K_PASS * g : K_PASS * (g + 1)].bitcast(F32)[:, u:256:2],
+                    t[:],
+                )
+
+        def adj_quant(q, passes=range(PASSES)):
+            for g in passes:
+                nc.vector.quantize_mx(
+                    out=a_codes[:, q, g, :].bitcast(E4M3X4), scales=a_plane[:, q, g, :], in_=a_grp[q, g][:]
+                )
+
+        accs = {}
+
+        def stage2(q, js=(0, 1)):
+            for j in js:
+                acc = ps2.tile([P, HID], F32, name="acc")
+                accs[q, j] = acc
+                for g in range(PASSES):
+                    cols = slice(P * j, P * (j + 1))
+                    nc.tensor.matmul_mx(
+                        out=acc[:],
+                        lhsT=a_codes[:, q, g, cols].bitcast(E4M3X4),
+                        lhsT_scale=a_plane[:, q, g, cols],
+                        rhs=s_codes[:, g, :].bitcast(E4M3X4),
+                        rhs_scale=s_plane[:, g, :],
+                        start=(g == 0),
+                        stop=(g == PASSES - 1),
+                    )
+
+        out_t = {}
+
+        def finish(q, j, parts=1):
+            rows = out[2 * P * q : 2 * P * (q + 1), :].rearrange("(m j) h -> m j h", j=2)
+            if j == 0:
+                t = outs.tile([P, 2, HID], F32, name="out_tile")
+                out_t[q] = t
+            w = HID // parts
+            for c in range(parts):
+                cols = slice(w * c, w * (c + 1))
+                part = out_t[q][:, j, cols]
+                nc.vector.tensor_tensor(out=part, in0=accs[q, j][:, cols], in1=bias[:, cols], op=ALU.add)
+                nc.scalar.activation(out=part, in_=part, func=ACT.Relu)
+                if q == PAIRS - 1:
+                    nc.sync.dma_start(out=rows[:, j, cols], in_=part)
+            if q < PAIRS - 1 and j == 1:
+                nc.sync.dma_start(out=rows, in_=out_t[q][:])
+
+        with tc.manual_schedule():
+            nc.gpsimd.memset(w_plane[:].bitcast(I32), 0)
+            for g in range(PASSES):
+                load_scale(g)
+                load_adj(0, g, PASSES)
+            load_x(0)
+            load_w()
+            load_x(1)
+            load_adj(1)
+            load_x(2)
+            load_adj(2)
+            nc.sync.dma_start(out=bias[:], in_=b1.partition_broadcast(P))
+            for q in range(3, PAIRS):
+                load_adj(q)
+
+            for g in range(PASSES):
+                adj_mult(0, g, PASSES)
+                adj_mult(1, g, PASSES)
+                adj_turn(0, [g])
+            x_turn(0)
+            adj_quant(0)
+            x_quant(0)
+            x_turn(1)
+            adj_mult(2)
+            stage1(0)
+            x_quant(1)
+            x_turn(2)
+            adj_mult(3)
+            stage1(1)
+            x_quant(2)
+            adj_mult(4)
+            s_quant(0)
+            stage1(2)
+            adj_mult(5)
+            adj_turn(1)
+            s_quant(1)
+            adj_mult(6)
+            s_quant(2)
+            adj_mult(7)
+            adj_quant(1)
+            stage2(0)
+            adj_turn(2)
+            adj_mult(8)
+            finish(0, 0)
+            finish(0, 1)
+            stage2(1)
+            adj_quant(2)
+            adj_turn(3)
+            adj_mult(9)
+            finish(1, 0)
+            finish(1, 1)
+            stage2(2)
+            adj_turn(4)
+            adj_mult(10)
+            adj_quant(3)
+            adj_mult(11)
+            stage2(3)
+            adj_turn(5)
+            finish(2, 0)
+            finish(2, 1)
+            adj_quant(4)
+            finish(3, 0)
+            stage2(4)
+            finish(3, 1)
+            adj_quant(5)
+            finish(4, 0)
+            stage2(5)
+            finish(4, 1)
+            finish(5, 0)
+            finish(5, 1, 2)

@@ -37,8 +37,6 @@ def tile_gcn_pa_w4_kernel(tc, x_init, adj_bytes, adj_scale, w_words, w_scales, b
         ps2 = ctx.enter_context(tc.psum_pool(name="ps2", bufs=3))
 
         ident = keep.tile([P, P], F32, name="ident")
-        make_identity(nc, ident[:])
-
         scale = keep.tile([P, NODES], F32, name="scale")
         bias = keep.tile([P, HID], BF16, name="bias")
         w_codes = keep.tile([P, 2 * HID], U8, name="w_codes", align_bytes=64)
@@ -65,17 +63,33 @@ def tile_gcn_pa_w4_kernel(tc, x_init, adj_bytes, adj_scale, w_words, w_scales, b
                 in_=adj_bytes[2 * P * q : 2 * P * (q + 1), cols].rearrange("(m j) k -> m j k", j=2),
             )
 
-        def load_x(g):
-            t = xraw.tile([P, 4, FEAT], BF16, name="x_raw_t")
-            nc.sync.dma_start(
-                out=t[:], in_=x_init[K_PASS * g : K_PASS * (g + 1), :].rearrange("(m t) f -> m t f", t=4)
-            )
-            x_raw[g] = t
+        def load_x(g, b=0, halves=1):
+            if b == 0:
+                t = xraw.tile([P, 4, FEAT], BF16, name="x_raw_t")
+                x_raw[g] = t
+            rows = x_init[K_PASS * g : K_PASS * (g + 1), :].rearrange("(m t) f -> m t f", t=4)
+            ts = slice(4 // halves * b, 4 // halves * (b + 1))
+            nc.sync.dma_start(out=x_raw[g][:, ts, :], in_=rows[:, ts, :])
 
-        def load_scale(g):
-            cols = slice(K_PASS * g, K_PASS * (g + 1))
-            nc.sync.dma_start(
-                out=scale[:, cols], in_=adj_scale[:, cols].rearrange("o k -> (o k)").partition_broadcast(P)
+        scale_rows = keep.tile([P, P], F32, name="scale_rows")
+        scale_cols = keep.tile([P, NODES // P], F32, name="scale_cols")
+
+        def load_scale():
+            n = NODES // P
+            nc.sync.dma_start(out=scale_rows[0:n, :], in_=adj_scale.rearrange("o (c p) -> (o c) p", p=P))
+
+        def turn_scale():
+            bank = tp.tile([P, 4, P], F32, name="bank")
+            nc.tensor.transpose(bank[:, 0, :], scale_rows[:], ident[:])
+            nc.scalar.copy(out=scale_cols[:], in_=bank[:, 0, 0 : NODES // P])
+
+        def spread_scale(g):
+            bank = tp.tile([P, 4, P], F32, name="bank")
+            for c in range(4):
+                col = scale_cols[:, 4 * g + c : 4 * g + c + 1].to_broadcast([P, P])
+                nc.tensor.transpose(bank[:, c, :], col, ident[:])
+            nc.scalar.copy(
+                out=scale[:, K_PASS * g : K_PASS * (g + 1)], in_=bank[:].rearrange("p c n -> p (c n)")
             )
 
         def load_w():
@@ -109,14 +123,15 @@ def tile_gcn_pa_w4_kernel(tc, x_init, adj_bytes, adj_scale, w_words, w_scales, b
 
         x_grp = {}
 
-        def x_turn(g):
-            t = grp.tile([P, 4 * K_PASS], BF16, name="x_grp_t", align_bytes=64)
-            x_grp[g] = t
+        def x_turn(g, halves=(0, 1)):
+            if 0 in halves:
+                t = grp.tile([P, 4 * K_PASS], BF16, name="x_grp_t", align_bytes=64)
+                x_grp[g] = t
             words = x_raw[g][:].rearrange("p t f -> p (t f)").bitcast(F32)
-            for b in range(2):
+            for b in halves:
                 turn(
                     lambda a, u: words[:, 256 * (2 * b + a) + u : 256 * (2 * b + a + 1) : 2],
-                    t[:, 1024 * b : 1024 * (b + 1)],
+                    x_grp[g][:, 1024 * b : 1024 * (b + 1)],
                 )
 
         def x_quant(g):
@@ -202,27 +217,35 @@ def tile_gcn_pa_w4_kernel(tc, x_init, adj_bytes, adj_scale, w_words, w_scales, b
                 nc.sync.dma_start(out=rows, in_=out_t[q][:])
 
         with tc.manual_schedule():
+            nc.gpsimd.memset(scale_rows[:], 0.0)
             nc.gpsimd.memset(w_plane[:].bitcast(I32), 0)
-            for g in range(PASSES):
-                load_scale(g)
-                load_adj(0, g, PASSES)
-            load_x(0)
+            make_identity(nc, ident[:])
+            load_scale()
+            load_adj(0, 0, PASSES)
+            load_x(0, 0, 2)
+            load_adj(0, 1, PASSES)
+            load_x(0, 1, 2)
+            load_adj(0, 2, PASSES)
             load_w()
             load_x(1)
             load_adj(1)
             load_x(2)
-            load_adj(2)
-            nc.sync.dma_start(out=bias[:], in_=b1.partition_broadcast(P))
-            for q in range(3, PAIRS):
+            for q in range(2, PAIRS):
                 load_adj(q)
+            nc.sync.dma_start(out=bias[:], in_=b1.partition_broadcast(P))
 
+            turn_scale()
+            spread_scale(0)
+            x_turn(0, [0])
+            spread_scale(1)
+            spread_scale(2)
             for g in range(PASSES):
                 adj_mult(0, g, PASSES)
                 adj_mult(1, g, PASSES)
-                adj_turn(0, [g])
-            x_turn(0)
-            adj_quant(0)
+            x_turn(0, [1])
+            adj_turn(0)
             x_quant(0)
+            adj_quant(0)
             x_turn(1)
             adj_mult(2)
             stage1(0)

@@ -17,9 +17,10 @@ ALU = mybir.AluOpType
 ACT = mybir.ActivationFunctionType
 
 P = 128
-K_PASS = 512
+K_PASS = 4 * P
 PASSES = NODES // K_PASS
-PAIRS = NODES // (2 * P)
+PAIR_ROWS = 2 * P
+PAIRS = NODES // PAIR_ROWS
 
 FLOPS = 2 * NODES * FEAT * HID + 2 * NODES * NODES * HID
 
@@ -28,82 +29,84 @@ def tile_gcn_pa_w4_kernel(tc, x_init, adj_bytes, adj_scale, w_words, w_scales, b
     nc = tc.nc
     with ExitStack() as ctx:
         keep = ctx.enter_context(tc.tile_pool(name="keep", bufs=1))
-        raw = ctx.enter_context(tc.tile_pool(name="raw", bufs=6))
-        xraw = ctx.enter_context(tc.tile_pool(name="xraw", bufs=3))
-        grp = ctx.enter_context(tc.tile_pool(name="grp", bufs=3))
-        agrp = ctx.enter_context(tc.tile_pool(name="agrp", bufs=6))
-        outs = ctx.enter_context(tc.tile_pool(name="outs", bufs=4))
+        a_in = ctx.enter_context(tc.tile_pool(name="a_in", bufs=PAIRS))
+        x_in = ctx.enter_context(tc.tile_pool(name="x_in", bufs=PASSES))
+        wide = ctx.enter_context(tc.tile_pool(name="wide", bufs=3))
+        narrow = ctx.enter_context(tc.tile_pool(name="narrow", bufs=6))
+        flipped = ctx.enter_context(tc.tile_pool(name="flipped", bufs=2))
+        results = ctx.enter_context(tc.tile_pool(name="results", bufs=PAIRS))
         tp = ctx.enter_context(tc.psum_pool(name="tp", bufs=5))
-        ps2 = ctx.enter_context(tc.psum_pool(name="ps2", bufs=3))
+        sums = ctx.enter_context(tc.psum_pool(name="sums", bufs=3))
 
         ident = keep.tile([P, P], F32, name="ident")
+        scale_cols = keep.tile([P, PASSES, 4], F32, name="scale_cols")
         scale = keep.tile([P, NODES], F32, name="scale")
         bias = keep.tile([P, HID], BF16, name="bias")
+        bias_rows = keep.tile([P, P], BF16, name="bias_rows")
+        bias_rows_f32 = keep.tile([P, P], F32, name="bias_rows_f32")
+        bias_col = keep.tile([P, 4], F32, name="bias_col")
         w_codes = keep.tile([P, 2 * HID], U8, name="w_codes", align_bytes=64)
         w_plane = keep.tile([P, HID], U8, name="w_plane", align_bytes=64)
         x_codes = keep.tile([P, PASSES, K_PASS], U32, name="x_codes", align_bytes=64)
         x_plane = keep.tile([P, PASSES, K_PASS], U8, name="x_plane", align_bytes=64)
         s_codes = keep.tile([P, PASSES, HID], U32, name="s_codes", align_bytes=64)
         s_plane = keep.tile([P, PASSES, HID], U8, name="s_plane", align_bytes=64)
-        a_codes = keep.tile([P, PAIRS, PASSES, 2 * P], U32, name="a_codes", align_bytes=64)
-        a_plane = keep.tile([P, PAIRS, PASSES, 2 * P], U8, name="a_plane", align_bytes=64)
+        a_codes = keep.tile([P, PAIRS, PASSES, PAIR_ROWS], U32, name="a_codes", align_bytes=64)
+        a_plane = keep.tile([P, PAIRS, PASSES, PAIR_ROWS], U8, name="a_plane", align_bytes=64)
         a_vals = keep.tile([P, PAIRS, 2, NODES], BF16, name="a_vals")
 
-        a_raw = {}
-        x_raw = {}
+        a_raw, x_raw, x_grp, s_grp, a_grp = {}, {}, {}, {}, {}
+        acc, flip, result = {}, {}, {}
+
+        def load_scale():
+            nc.sync.dma_start(
+                out=scale_cols[:], in_=adj_scale.rearrange("o (g p t) -> p (o g) t", p=P, t=4)
+            )
 
         def load_adj(q, c=0, pieces=1):
             if c == 0:
-                t = raw.tile([P, 2, NODES], U8, name="a_raw_t")
-                a_raw[q] = t
-            w = NODES // pieces
-            cols = slice(w * c, w * (c + 1))
-            nc.sync.dma_start(
-                out=a_raw[q][:, :, cols],
-                in_=adj_bytes[2 * P * q : 2 * P * (q + 1), cols].rearrange("(m j) k -> m j k", j=2),
-            )
+                raw = a_in.tile([P, 2, NODES], U8, name="raw")
+                a_raw[q] = raw
+            cols = slice(NODES // pieces * c, NODES // pieces * (c + 1))
+            rows = adj_bytes[PAIR_ROWS * q : PAIR_ROWS * (q + 1), cols]
+            nc.sync.dma_start(out=a_raw[q][:, :, cols], in_=rows.rearrange("(m j) k -> m j k", j=2))
 
-        def load_x(g, b=0, halves=1):
-            if b == 0:
-                t = xraw.tile([P, 4, FEAT], BF16, name="x_raw_t")
-                x_raw[g] = t
+        def load_x(g, c=0, pieces=1):
+            if c == 0:
+                x = x_in.tile([P, 4, FEAT], BF16, name="x")
+                x_raw[g] = x
+            ts = slice(4 // pieces * c, 4 // pieces * (c + 1))
             rows = x_init[K_PASS * g : K_PASS * (g + 1), :].rearrange("(m t) f -> m t f", t=4)
-            ts = slice(4 // halves * b, 4 // halves * (b + 1))
             nc.sync.dma_start(out=x_raw[g][:, ts, :], in_=rows[:, ts, :])
 
-        scale_rows = keep.tile([P, P], F32, name="scale_rows")
-        scale_cols = keep.tile([P, NODES // P], F32, name="scale_cols")
+        def load_w_codes():
+            nc.sync.dma_start(out=w_codes[:].bitcast(I32), in_=w_words[0].bitcast(I32))
 
-        def load_scale():
-            n = NODES // P
-            nc.sync.dma_start(out=scale_rows[0:n, :], in_=adj_scale.rearrange("o (c p) -> (o c) p", p=P))
-
-        def turn_scale():
-            bank = tp.tile([P, 4, P], F32, name="bank")
-            nc.tensor.transpose(bank[:, 0, :], scale_rows[:], ident[:])
-            nc.scalar.copy(out=scale_cols[:], in_=bank[:, 0, 0 : NODES // P])
+        def load_w_plane():
+            for quad in range(4):
+                nc.sync.dma_start(
+                    out=w_plane[32 * quad : 32 * quad + 4, :].bitcast(I32),
+                    in_=w_scales[0, 4 * quad : 4 * quad + 4, :].bitcast(I32),
+                )
 
         def spread_scale(g):
             bank = tp.tile([P, 4, P], F32, name="bank")
-            for c in range(4):
-                col = scale_cols[:, 4 * g + c : 4 * g + c + 1].to_broadcast([P, P])
-                nc.tensor.transpose(bank[:, c, :], col, ident[:])
+            for t in range(4):
+                nc.tensor.transpose(bank[:, t, :], scale_cols[:, g, t : t + 1].to_broadcast([P, P]), ident[:])
             nc.scalar.copy(
-                out=scale[:, K_PASS * g : K_PASS * (g + 1)], in_=bank[:].rearrange("p c n -> p (c n)")
+                out=scale[:, K_PASS * g : K_PASS * (g + 1)].rearrange("p (n t) -> p n t", t=4),
+                in_=bank[:].rearrange("p t n -> p n t"),
             )
 
-        def load_w():
-            nc.sync.dma_start(out=w_codes[:].bitcast(I32), in_=w_words[0].bitcast(I32))
-            for q in range(4):
-                nc.sync.dma_start(
-                    out=w_plane[32 * q : 32 * q + 4, :].bitcast(I32),
-                    in_=w_scales[0, 4 * q : 4 * q + 4, :].bitcast(I32),
-                )
+        def turn_bias():
+            nc.gpsimd.tensor_copy(out=bias_rows_f32[:], in_=bias_rows[:])
+            bank = tp.tile([P, 4, P], F32, name="bank")
+            nc.tensor.transpose(bank[:, 0, :], bias_rows_f32[:], ident[:])
+            nc.scalar.copy(out=bias_col[:], in_=bank[:, 0, 0:4])
 
         def adj_mult(i, c=0, pieces=1):
             q, j = divmod(i, 2)
-            w = NODES // pieces
-            cols = slice(w * c, w * (c + 1))
+            cols = slice(NODES // pieces * c, NODES // pieces * (c + 1))
             nc.vector.tensor_tensor(
                 out=a_vals[:, q, j, cols],
                 in0=a_raw[q][:, j, cols].bitcast(E4M3),
@@ -111,186 +114,213 @@ def tile_gcn_pa_w4_kernel(tc, x_init, adj_bytes, adj_scale, w_words, w_scales, b
                 op=ALU.mult,
             )
 
-        def turn(src_words, dst):
+        def turn(runs, grouped):
             bank = tp.tile([P, 4, P], F32, name="bank")
             for a in range(2):
                 for u in range(2):
-                    nc.tensor.transpose(bank[:, 2 * a + u, :], src_words(a, u), ident[:])
+                    nc.tensor.transpose(bank[:, 2 * a + u, :], runs[a][:, u : 2 * P : 2], ident[:])
             nc.scalar.copy(
-                out=dst.bitcast(F32).rearrange("p (a m u) -> p a m u", a=2, u=2),
+                out=grouped.bitcast(F32).rearrange("p (a m u) -> p a m u", a=2, u=2),
                 in_=bank[:].rearrange("p (a u) m -> p a m u", a=2),
             )
 
-        x_grp = {}
-
-        def x_turn(g, halves=(0, 1)):
-            if 0 in halves:
-                t = grp.tile([P, 4 * K_PASS], BF16, name="x_grp_t", align_bytes=64)
-                x_grp[g] = t
-            words = x_raw[g][:].rearrange("p t f -> p (t f)").bitcast(F32)
-            for b in halves:
-                turn(
-                    lambda a, u: words[:, 256 * (2 * b + a) + u : 256 * (2 * b + a + 1) : 2],
-                    x_grp[g][:, 1024 * b : 1024 * (b + 1)],
-                )
+        def x_turn(g, b):
+            if b == 0:
+                grouped = wide.tile([P, 4 * K_PASS], BF16, name="x_grouped", align_bytes=64)
+                x_grp[g] = grouped
+            runs = [x_raw[g][:, 2 * b + a, :].bitcast(F32) for a in range(2)]
+            turn(runs, x_grp[g][:, 8 * P * b : 8 * P * (b + 1)])
 
         def x_quant(g):
             nc.vector.quantize_mx(out=x_codes[:, g, :].bitcast(E4M3X4), scales=x_plane[:, g, :], in_=x_grp[g][:])
 
-        s_grp = {}
-
         def stage1(g):
-            t = grp.tile([P, 4 * HID], BF16, name="s_grp_t", align_bytes=64)
-            s_grp[g] = t
-            for c in range(4):
+            grouped = wide.tile([P, 4 * HID], BF16, name="s_grouped", align_bytes=64)
+            s_grp[g] = grouped
+            for c in range(HID // P):
                 bank = tp.tile([P, 4, P], F32, name="bank")
-                for k in range(4):
-                    cols = slice(P * k, P * (k + 1))
+                for t in range(4):
+                    cols = slice(P * t, P * (t + 1))
                     nc.tensor.matmul_mx(
-                        out=bank[:, k, :],
+                        out=bank[:, t, :],
                         lhsT=x_codes[:, g, cols].bitcast(E4M3X4),
                         lhsT_scale=x_plane[:, g, cols],
-                        rhs=w_codes[:, 256 * c : 256 * (c + 1)].bitcast(E2M1X4),
+                        rhs=w_codes[:, 2 * P * c : 2 * P * (c + 1)].bitcast(E2M1X4),
                         rhs_scale=w_plane[:, P * c : P * (c + 1)],
                         start=True,
                         stop=True,
                     )
                 nc.scalar.copy(
-                    out=t[:, 512 * c : 512 * (c + 1)].rearrange("p (n t) -> p n t", t=4),
+                    out=grouped[:, 4 * P * c : 4 * P * (c + 1)].rearrange("p (n t) -> p n t", t=4),
                     in_=bank[:].rearrange("p t n -> p n t"),
                 )
 
         def s_quant(g):
             nc.vector.quantize_mx(out=s_codes[:, g, :].bitcast(E4M3X4), scales=s_plane[:, g, :], in_=s_grp[g][:])
 
-        a_grp = {}
+        def adj_turn(q):
+            for g in range(PASSES):
+                grouped = narrow.tile([P, 4 * PAIR_ROWS], BF16, name="a_grouped", align_bytes=64)
+                a_grp[q, g] = grouped
+                runs = [a_vals[:, q, j, K_PASS * g : K_PASS * (g + 1)].bitcast(F32) for j in range(2)]
+                turn(runs, grouped[:])
 
-        def adj_turn(q, passes=range(PASSES)):
-            for g in passes:
-                t = agrp.tile([P, 8 * P], BF16, name="a_grp_t", align_bytes=64)
-                a_grp[q, g] = t
-                turn(
-                    lambda a, u: a_vals[:, q, a, K_PASS * g : K_PASS * (g + 1)].bitcast(F32)[:, u:256:2],
-                    t[:],
-                )
-
-        def adj_quant(q, passes=range(PASSES)):
-            for g in passes:
+        def adj_quant(q):
+            for g in range(PASSES):
                 nc.vector.quantize_mx(
                     out=a_codes[:, q, g, :].bitcast(E4M3X4), scales=a_plane[:, q, g, :], in_=a_grp[q, g][:]
                 )
 
-        accs = {}
+        def out_rows(q):
+            return out[PAIR_ROWS * q : PAIR_ROWS * (q + 1), :].rearrange("(m j) h -> m j h", j=2)
 
-        def stage2(q, js=(0, 1)):
-            for j in js:
-                acc = ps2.tile([P, HID], F32, name="acc")
-                accs[q, j] = acc
+        def stage2(q, j):
+            total = sums.tile([P, HID], F32, name="total")
+            acc[q, j] = total
+            for g in range(PASSES):
+                cols = slice(P * j, P * (j + 1))
+                nc.tensor.matmul_mx(
+                    out=total[:],
+                    lhsT=a_codes[:, q, g, cols].bitcast(E4M3X4),
+                    lhsT_scale=a_plane[:, q, g, cols],
+                    rhs=s_codes[:, g, :].bitcast(E4M3X4),
+                    rhs_scale=s_plane[:, g, :],
+                    start=(g == 0),
+                    stop=(g == PASSES - 1),
+                )
+
+        def finish(q, j, pieces=1):
+            if j == 0:
+                res = results.tile([P, 2, HID], F32, name="res")
+                result[q] = res
+            for c in range(pieces):
+                cols = slice(HID // pieces * c, HID // pieces * (c + 1))
+                part = result[q][:, j, cols]
+                nc.vector.tensor_tensor(out=part, in0=acc[q, j][:, cols], in1=bias[:, cols], op=ALU.add)
+                nc.scalar.activation(out=part, in_=part, func=ACT.Relu)
+                if q == PAIRS - 1:
+                    nc.sync.dma_start(out=out_rows(q)[:, j, cols], in_=part)
+            if q < PAIRS - 1 and j == 1:
+                nc.sync.dma_start(out=out_rows(q), in_=result[q][:])
+
+        def stage2_flipped(q, h):
+            if h == 0:
+                flat = flipped.tile([P, 4, PAIR_ROWS], F32, name="flat")
+                flip[q] = flat
+            total = sums.tile([P, HID], F32, name="total")
+            halves = [total[:, PAIR_ROWS * i : PAIR_ROWS * (i + 1)] for i in range(2)]
+            for i in range(2):
+                cols = slice(P * (2 * h + i), P * (2 * h + i + 1))
                 for g in range(PASSES):
-                    cols = slice(P * j, P * (j + 1))
                     nc.tensor.matmul_mx(
-                        out=acc[:],
-                        lhsT=a_codes[:, q, g, cols].bitcast(E4M3X4),
-                        lhsT_scale=a_plane[:, q, g, cols],
-                        rhs=s_codes[:, g, :].bitcast(E4M3X4),
-                        rhs_scale=s_plane[:, g, :],
+                        out=halves[i],
+                        lhsT=s_codes[:, g, cols].bitcast(E4M3X4),
+                        lhsT_scale=s_plane[:, g, cols],
+                        rhs=a_codes[:, q, g, :].bitcast(E4M3X4),
+                        rhs_scale=a_plane[:, q, g, :],
                         start=(g == 0),
                         stop=(g == PASSES - 1),
                     )
+            for i in range(2):
+                c = 2 * h + i
+                nc.scalar.activation(
+                    out=flip[q][:, c, :], in_=halves[i], func=ACT.Relu, bias=bias_col[:, c : c + 1]
+                )
 
-        out_t = {}
-
-        def finish(q, j, parts=1):
-            rows = out[2 * P * q : 2 * P * (q + 1), :].rearrange("(m j) h -> m j h", j=2)
+        def flip_back(q, j):
             if j == 0:
-                t = outs.tile([P, 2, HID], F32, name="out_tile")
-                out_t[q] = t
-            w = HID // parts
-            for c in range(parts):
-                cols = slice(w * c, w * (c + 1))
-                part = out_t[q][:, j, cols]
-                nc.vector.tensor_tensor(out=part, in0=accs[q, j][:, cols], in1=bias[:, cols], op=ALU.add)
-                nc.scalar.activation(out=part, in_=part, func=ACT.Relu)
-                if q == PAIRS - 1:
-                    nc.sync.dma_start(out=rows[:, j, cols], in_=part)
-            if q < PAIRS - 1 and j == 1:
-                nc.sync.dma_start(out=rows, in_=out_t[q][:])
+                res = results.tile([P, 2, HID], F32, name="res")
+                result[q] = res
+            bank = tp.tile([P, 4, P], F32, name="bank")
+            for c in range(4):
+                nc.tensor.transpose(bank[:, c, :], flip[q][:, c, P * j : P * (j + 1)], ident[:])
+            nc.scalar.copy(out=result[q][:, j, :], in_=bank[:].rearrange("p c m -> p (c m)"))
+            if j == 1:
+                nc.sync.dma_start(out=out_rows(q), in_=result[q][:])
 
         with tc.manual_schedule():
-            nc.gpsimd.memset(scale_rows[:], 0.0)
-            nc.gpsimd.memset(w_plane[:].bitcast(I32), 0)
             make_identity(nc, ident[:])
+            nc.gpsimd.memset(bias_rows[:], 0.0)
+            nc.gpsimd.memset(w_plane[:].bitcast(I32), 0)
             load_scale()
-            load_adj(0, 0, PASSES)
+            load_adj(0, 0, 3)
             load_x(0, 0, 2)
-            load_adj(0, 1, PASSES)
+            load_adj(0, 1, 3)
             load_x(0, 1, 2)
-            load_adj(0, 2, PASSES)
-            load_w()
+            load_adj(0, 2, 3)
+            load_w_codes()
             load_x(1)
+            nc.sync.dma_start(out=bias_rows[0:4, :], in_=b1.rearrange("(c m) -> c m", m=P))
+            load_w_plane()
             load_adj(1)
             load_x(2)
             for q in range(2, PAIRS):
                 load_adj(q)
             nc.sync.dma_start(out=bias[:], in_=b1.partition_broadcast(P))
 
-            turn_scale()
-            spread_scale(0)
-            x_turn(0, [0])
-            spread_scale(1)
-            spread_scale(2)
             for g in range(PASSES):
-                adj_mult(0, g, PASSES)
-                adj_mult(1, g, PASSES)
-            x_turn(0, [1])
+                spread_scale(g)
+            for b in range(2):
+                x_turn(0, b)
+            for g in range(PASSES):
+                for i in range(2):
+                    adj_mult(i, g, PASSES)
+            x_turn(1, 0)
+            adj_mult(2)
             adj_turn(0)
             x_quant(0)
-            adj_quant(0)
-            x_turn(1)
-            adj_mult(2)
-            stage1(0)
-            x_quant(1)
-            x_turn(2)
+            x_turn(1, 1)
             adj_mult(3)
-            stage1(1)
+            x_turn(2, 0)
+            x_turn(2, 1)
+            x_quant(1)
             x_quant(2)
             adj_mult(4)
-            s_quant(0)
-            stage1(2)
             adj_mult(5)
-            adj_turn(1)
+            for g in range(PASSES):
+                stage1(g)
+            turn_bias()
+            adj_quant(0)
+            s_quant(0)
             s_quant(1)
-            adj_mult(6)
+            adj_turn(1)
             s_quant(2)
-            adj_mult(7)
-            adj_quant(1)
-            stage2(0)
             adj_turn(2)
-            adj_mult(8)
-            finish(0, 0)
-            finish(0, 1)
-            stage2(1)
+            stage2_flipped(0, 0)
+            stage2_flipped(0, 1)
+            adj_mult(6)
+            adj_quant(1)
             adj_quant(2)
-            adj_turn(3)
+            adj_mult(7)
+            stage2_flipped(1, 0)
+            stage2(2, 0)
+            stage2_flipped(1, 1)
+            stage2(2, 1)
+            adj_mult(8)
             adj_mult(9)
-            finish(1, 0)
-            finish(1, 1)
-            stage2(2)
-            adj_turn(4)
-            adj_mult(10)
-            adj_quant(3)
-            adj_mult(11)
-            stage2(3)
-            adj_turn(5)
+            adj_turn(3)
+            flip_back(0, 0)
             finish(2, 0)
-            finish(2, 1)
+            flip_back(0, 1)
+            adj_turn(4)
+            adj_quant(3)
+            stage2(3, 0)
+            stage2(3, 1)
+            adj_mult(10)
+            adj_mult(11)
+            flip_back(1, 0)
+            flip_back(1, 1)
+            adj_turn(5)
             adj_quant(4)
+            finish(2, 1)
             finish(3, 0)
-            stage2(4)
-            finish(3, 1)
             adj_quant(5)
+            stage2(4, 0)
+            finish(3, 1)
             finish(4, 0)
-            stage2(5)
+            stage2(4, 1)
             finish(4, 1)
+            stage2(5, 0)
             finish(5, 0)
+            stage2(5, 1)
             finish(5, 1, 2)

@@ -32,8 +32,8 @@ def tile_gcn_pa_w4_kernel(tc, x_init, adj_bytes, adj_scale, w_words, w_scales, b
         a_in = ctx.enter_context(tc.tile_pool(name="a_in", bufs=PAIRS))
         x_in = ctx.enter_context(tc.tile_pool(name="x_in", bufs=PASSES))
         wide = ctx.enter_context(tc.tile_pool(name="wide", bufs=3))
-        narrow = ctx.enter_context(tc.tile_pool(name="narrow", bufs=6))
-        flipped = ctx.enter_context(tc.tile_pool(name="flipped", bufs=2))
+        narrow = ctx.enter_context(tc.tile_pool(name="narrow", bufs=3))
+        flipped = ctx.enter_context(tc.tile_pool(name="flipped", bufs=3))
         results = ctx.enter_context(tc.tile_pool(name="results", bufs=PAIRS))
         tp = ctx.enter_context(tc.psum_pool(name="tp", bufs=5))
         sums = ctx.enter_context(tc.psum_pool(name="sums", bufs=3))
@@ -63,11 +63,11 @@ def tile_gcn_pa_w4_kernel(tc, x_init, adj_bytes, adj_scale, w_words, w_scales, b
                 out=scale_cols[:], in_=adj_scale.rearrange("o (g p t) -> p (o g) t", p=P, t=4)
             )
 
-        def load_adj(q, c=0, pieces=1):
-            if c == 0:
+        def load_adj(q, first=0, last=NODES):
+            if first == 0:
                 raw = a_in.tile([P, 2, NODES], U8, name="raw")
                 a_raw[q] = raw
-            cols = slice(NODES // pieces * c, NODES // pieces * (c + 1))
+            cols = slice(first, last)
             rows = adj_bytes[PAIR_ROWS * q : PAIR_ROWS * (q + 1), cols]
             nc.sync.dma_start(out=a_raw[q][:, :, cols], in_=rows.rearrange("(m j) k -> m j k", j=2))
 
@@ -93,10 +93,12 @@ def tile_gcn_pa_w4_kernel(tc, x_init, adj_bytes, adj_scale, w_words, w_scales, b
             bank = tp.tile([P, 4, P], F32, name="bank")
             for t in range(4):
                 nc.tensor.transpose(bank[:, t, :], scale_cols[:, g, t : t + 1].to_broadcast([P, P]), ident[:])
-            nc.scalar.copy(
-                out=scale[:, K_PASS * g : K_PASS * (g + 1)].rearrange("p (n t) -> p n t", t=4),
-                in_=bank[:].rearrange("p t n -> p n t"),
-            )
+            out_ap = scale[:, K_PASS * g : K_PASS * (g + 1)].rearrange("p (n t) -> p n t", t=4)
+            in_ap = bank[:].rearrange("p t n -> p n t")
+            if g == 0:
+                nc.vector.tensor_copy(out=out_ap, in_=in_ap)
+            else:
+                nc.scalar.copy(out=out_ap, in_=in_ap)
 
         def turn_bias():
             nc.gpsimd.tensor_copy(out=bias_rows_f32[:], in_=bias_rows[:])
@@ -158,17 +160,19 @@ def tile_gcn_pa_w4_kernel(tc, x_init, adj_bytes, adj_scale, w_words, w_scales, b
         def s_quant(g):
             nc.vector.quantize_mx(out=s_codes[:, g, :].bitcast(E4M3X4), scales=s_plane[:, g, :], in_=s_grp[g][:])
 
-        def adj_turn(q):
-            for g in range(PASSES):
-                grouped = narrow.tile([P, 4 * PAIR_ROWS], BF16, name="a_grouped", align_bytes=64)
-                a_grp[q, g] = grouped
-                runs = [a_vals[:, q, j, K_PASS * g : K_PASS * (g + 1)].bitcast(F32) for j in range(2)]
-                turn(runs, grouped[:])
+        def adj_turn(q, g):
+            if g == 0:
+                grouped = narrow.tile([P, PASSES, 4 * PAIR_ROWS], BF16, name="a_grouped", align_bytes=64)
+                a_grp[q] = grouped
+            runs = [a_vals[:, q, j, K_PASS * g : K_PASS * (g + 1)].bitcast(F32) for j in range(2)]
+            turn(runs, a_grp[q][:, g, :])
 
         def adj_quant(q):
-            for g in range(PASSES):
+            for gs in (slice(0, 2), slice(2, 3)):
                 nc.vector.quantize_mx(
-                    out=a_codes[:, q, g, :].bitcast(E4M3X4), scales=a_plane[:, q, g, :], in_=a_grp[q, g][:]
+                    out=a_codes[:, q, gs, :].rearrange("p g r -> p (g r)").bitcast(E4M3X4),
+                    scales=a_plane[:, q, gs, :].rearrange("p g r -> p (g r)"),
+                    in_=a_grp[q][:, gs, :].rearrange("p g r -> p (g r)"),
                 )
 
         def out_rows(q):
@@ -198,10 +202,7 @@ def tile_gcn_pa_w4_kernel(tc, x_init, adj_bytes, adj_scale, w_words, w_scales, b
                 part = result[q][:, j, cols]
                 nc.vector.tensor_tensor(out=part, in0=acc[q, j][:, cols], in1=bias[:, cols], op=ALU.add)
                 nc.scalar.activation(out=part, in_=part, func=ACT.Relu)
-                if q == PAIRS - 1:
-                    nc.sync.dma_start(out=out_rows(q)[:, j, cols], in_=part)
-            if q < PAIRS - 1 and j == 1:
-                nc.sync.dma_start(out=out_rows(q), in_=result[q][:])
+                nc.sync.dma_start(out=out_rows(q)[:, j, cols], in_=part)
 
         def stage2_flipped(q, h):
             if h == 0:
@@ -235,88 +236,103 @@ def tile_gcn_pa_w4_kernel(tc, x_init, adj_bytes, adj_scale, w_words, w_scales, b
             for c in range(4):
                 nc.tensor.transpose(bank[:, c, :], flip[q][:, c, P * j : P * (j + 1)], ident[:])
             nc.scalar.copy(out=result[q][:, j, :], in_=bank[:].rearrange("p c m -> p (c m)"))
-            if j == 1:
-                nc.sync.dma_start(out=out_rows(q), in_=result[q][:])
+            nc.sync.dma_start(out=out_rows(q)[:, j, :], in_=result[q][:, j, :])
 
         with tc.manual_schedule():
             make_identity(nc, ident[:])
-            nc.gpsimd.memset(bias_rows[:], 0.0)
             nc.gpsimd.memset(w_plane[:].bitcast(I32), 0)
+            nc.gpsimd.memset(bias_rows[:], 0.0)
             load_scale()
-            load_adj(0, 0, 3)
+            load_adj(0, 0, K_PASS)
             load_x(0, 0, 2)
-            load_adj(0, 1, 3)
+            load_adj(0, K_PASS, NODES)
             load_x(0, 1, 2)
-            load_adj(0, 2, 3)
-            load_w_codes()
             load_x(1)
-            nc.sync.dma_start(out=bias_rows[0:4, :], in_=b1.rearrange("(c m) -> c m", m=P))
-            load_w_plane()
             load_adj(1)
             load_x(2)
+            load_w_codes()
+            load_w_plane()
+            nc.sync.dma_start(out=bias_rows[0:4, :], in_=b1.rearrange("(c m) -> c m", m=P))
             for q in range(2, PAIRS):
                 load_adj(q)
             nc.sync.dma_start(out=bias[:], in_=b1.partition_broadcast(P))
 
-            for g in range(PASSES):
-                spread_scale(g)
-            for b in range(2):
-                x_turn(0, b)
-            for g in range(PASSES):
-                for i in range(2):
-                    adj_mult(i, g, PASSES)
-            x_turn(1, 0)
-            adj_mult(2)
-            adj_turn(0)
+            spread_scale(0)
+            spread_scale(1)
+            x_turn(0, 0)
+            spread_scale(2)
+            adj_mult(0, 0, 3)
+            adj_mult(1, 0, 3)
+            adj_turn(0, 0)
+            x_turn(0, 1)
+            adj_mult(0, 1, 3)
+            adj_mult(1, 1, 3)
+            adj_mult(0, 2, 3)
+            adj_mult(1, 2, 3)
             x_quant(0)
+            x_turn(1, 0)
             x_turn(1, 1)
-            adj_mult(3)
+            adj_turn(0, 1)
             x_turn(2, 0)
             x_turn(2, 1)
+            adj_mult(2)
             x_quant(1)
             x_quant(2)
+            stage1(0)
+            adj_mult(3)
+            s_quant(0)
+            stage1(1)
             adj_mult(4)
             adj_mult(5)
-            for g in range(PASSES):
-                stage1(g)
-            turn_bias()
-            adj_quant(0)
-            s_quant(0)
             s_quant(1)
-            adj_turn(1)
+            adj_turn(0, 2)
+            stage1(2)
+            turn_bias()
+            adj_turn(1, 0)
+            adj_turn(1, 1)
+            adj_turn(1, 2)
+            adj_quant(0)
+            adj_turn(2, 0)
+            adj_turn(2, 1)
+            adj_turn(2, 2)
             s_quant(2)
-            adj_turn(2)
+            adj_quant(1)
             stage2_flipped(0, 0)
             stage2_flipped(0, 1)
             adj_mult(6)
-            adj_quant(1)
             adj_quant(2)
             adj_mult(7)
             stage2_flipped(1, 0)
-            stage2(2, 0)
             stage2_flipped(1, 1)
-            stage2(2, 1)
+            stage2_flipped(2, 0)
             adj_mult(8)
-            adj_mult(9)
-            adj_turn(3)
+            stage2_flipped(2, 1)
+            adj_turn(3, 0)
+            adj_turn(3, 1)
+            adj_turn(3, 2)
             flip_back(0, 0)
-            finish(2, 0)
             flip_back(0, 1)
-            adj_turn(4)
+            adj_mult(9)
             adj_quant(3)
-            stage2(3, 0)
-            stage2(3, 1)
-            adj_mult(10)
-            adj_mult(11)
             flip_back(1, 0)
             flip_back(1, 1)
-            adj_turn(5)
+            adj_turn(4, 0)
+            adj_turn(4, 1)
+            adj_turn(4, 2)
+            adj_mult(10)
+            stage2(3, 0)
+            adj_mult(11)
+            stage2(3, 1)
             adj_quant(4)
-            finish(2, 1)
-            finish(3, 0)
-            adj_quant(5)
+            flip_back(2, 0)
+            flip_back(2, 1)
+            adj_turn(5, 0)
+            adj_turn(5, 1)
+            adj_turn(5, 2)
             stage2(4, 0)
+            finish(3, 0)
             finish(3, 1)
+            adj_quant(5)
             finish(4, 0)
             stage2(4, 1)
             finish(4, 1)

@@ -33,13 +33,13 @@ def tile_gcn_pa_w4_kernel(tc, x_init, adj_bytes, adj_scale, w_words, w_scales, b
         x_in = ctx.enter_context(tc.tile_pool(name="x_in", bufs=PASSES))
         wide = ctx.enter_context(tc.tile_pool(name="wide", bufs=3))
         narrow = ctx.enter_context(tc.tile_pool(name="narrow", bufs=3))
-        flipped = ctx.enter_context(tc.tile_pool(name="flipped", bufs=3))
+        flipped = ctx.enter_context(tc.tile_pool(name="flipped", bufs=2))
         results = ctx.enter_context(tc.tile_pool(name="results", bufs=PAIRS))
         tp = ctx.enter_context(tc.psum_pool(name="tp", bufs=5))
         sums = ctx.enter_context(tc.psum_pool(name="sums", bufs=3))
 
         ident = keep.tile([P, P], F32, name="ident")
-        scale_cols = keep.tile([P, PASSES, 4], F32, name="scale_cols")
+        scale_cols = [keep.tile([P, 4], F32, name="scale_cols%d" % g) for g in range(PASSES)]
         scale = keep.tile([P, NODES], F32, name="scale")
         bias = keep.tile([P, HID], BF16, name="bias")
         bias_rows = keep.tile([P, P], BF16, name="bias_rows")
@@ -58,10 +58,9 @@ def tile_gcn_pa_w4_kernel(tc, x_init, adj_bytes, adj_scale, w_words, w_scales, b
         a_raw, x_raw, x_grp, s_grp, a_grp = {}, {}, {}, {}, {}
         acc, flip, result = {}, {}, {}
 
-        def load_scale():
-            nc.sync.dma_start(
-                out=scale_cols[:], in_=adj_scale.rearrange("o (g p t) -> p (o g) t", p=P, t=4)
-            )
+        def load_scale(g):
+            by_partition = adj_scale[:, K_PASS * g : K_PASS * (g + 1)].rearrange("o (p t) -> p (o t)", t=4)
+            nc.sync.dma_start(out=scale_cols[g][:], in_=by_partition)
 
         def load_adj(q, first=0, last=NODES):
             if first == 0:
@@ -92,7 +91,7 @@ def tile_gcn_pa_w4_kernel(tc, x_init, adj_bytes, adj_scale, w_words, w_scales, b
         def spread_scale(g):
             bank = tp.tile([P, 4, P], F32, name="bank")
             for t in range(4):
-                nc.tensor.transpose(bank[:, t, :], scale_cols[:, g, t : t + 1].to_broadcast([P, P]), ident[:])
+                nc.tensor.transpose(bank[:, t, :], scale_cols[g][:, t : t + 1].to_broadcast([P, P]), ident[:])
             out_ap = scale[:, K_PASS * g : K_PASS * (g + 1)].rearrange("p (n t) -> p n t", t=4)
             in_ap = bank[:].rearrange("p t n -> p n t")
             if g == 0:
@@ -101,7 +100,7 @@ def tile_gcn_pa_w4_kernel(tc, x_init, adj_bytes, adj_scale, w_words, w_scales, b
                 nc.scalar.copy(out=out_ap, in_=in_ap)
 
         def turn_bias():
-            nc.gpsimd.tensor_copy(out=bias_rows_f32[:], in_=bias_rows[:])
+            nc.vector.tensor_copy(out=bias_rows_f32[:], in_=bias_rows[:])
             bank = tp.tile([P, 4, P], F32, name="bank")
             nc.tensor.transpose(bank[:, 0, :], bias_rows_f32[:], ident[:])
             nc.scalar.copy(out=bias_col[:], in_=bank[:, 0, 0:4])
@@ -242,8 +241,10 @@ def tile_gcn_pa_w4_kernel(tc, x_init, adj_bytes, adj_scale, w_words, w_scales, b
             make_identity(nc, ident[:])
             nc.gpsimd.memset(w_plane[:].bitcast(I32), 0)
             nc.gpsimd.memset(bias_rows[:], 0.0)
-            load_scale()
+            load_scale(0)
             load_adj(0, 0, K_PASS)
+            load_scale(1)
+            load_scale(2)
             load_x(0, 0, 2)
             load_adj(0, K_PASS, NODES)
             load_x(0, 1, 2)
@@ -259,84 +260,84 @@ def tile_gcn_pa_w4_kernel(tc, x_init, adj_bytes, adj_scale, w_words, w_scales, b
 
             spread_scale(0)
             spread_scale(1)
-            x_turn(0, 0)
             spread_scale(2)
             adj_mult(0, 0, 3)
             adj_mult(1, 0, 3)
-            adj_turn(0, 0)
+            x_turn(0, 0)
             x_turn(0, 1)
             adj_mult(0, 1, 3)
             adj_mult(1, 1, 3)
-            adj_mult(0, 2, 3)
-            adj_mult(1, 2, 3)
-            x_quant(0)
+            adj_turn(0, 0)
             x_turn(1, 0)
             x_turn(1, 1)
+            adj_mult(0, 2, 3)
+            adj_mult(1, 2, 3)
             adj_turn(0, 1)
+            x_quant(0)
             x_turn(2, 0)
             x_turn(2, 1)
             adj_mult(2)
             x_quant(1)
+            adj_turn(0, 2)
             x_quant(2)
             stage1(0)
             adj_mult(3)
-            s_quant(0)
             stage1(1)
             adj_mult(4)
-            adj_mult(5)
-            s_quant(1)
-            adj_turn(0, 2)
             stage1(2)
             turn_bias()
+            adj_mult(5)
+            adj_quant(0)
             adj_turn(1, 0)
             adj_turn(1, 1)
             adj_turn(1, 2)
-            adj_quant(0)
             adj_turn(2, 0)
             adj_turn(2, 1)
             adj_turn(2, 2)
+            s_quant(0)
+            s_quant(1)
             s_quant(2)
-            adj_quant(1)
-            stage2_flipped(0, 0)
-            stage2_flipped(0, 1)
             adj_mult(6)
+            adj_quant(1)
             adj_quant(2)
             adj_mult(7)
+            stage2_flipped(0, 0)
+            stage2_flipped(0, 1)
             stage2_flipped(1, 0)
             stage2_flipped(1, 1)
-            stage2_flipped(2, 0)
-            adj_mult(8)
-            stage2_flipped(2, 1)
+            stage2(2, 0)
+            flip_back(0, 0)
             adj_turn(3, 0)
             adj_turn(3, 1)
             adj_turn(3, 2)
-            flip_back(0, 0)
-            flip_back(0, 1)
+            flip_back(1, 0)
+            adj_mult(8)
             adj_mult(9)
             adj_quant(3)
-            flip_back(1, 0)
-            flip_back(1, 1)
+            stage2(2, 1)
+            finish(2, 0)
+            adj_mult(10)
+            flip_back(0, 1)
             adj_turn(4, 0)
             adj_turn(4, 1)
             adj_turn(4, 2)
-            adj_mult(10)
             stage2(3, 0)
-            adj_mult(11)
             stage2(3, 1)
-            adj_quant(4)
-            flip_back(2, 0)
-            flip_back(2, 1)
+            adj_mult(11)
+            flip_back(1, 1)
             adj_turn(5, 0)
             adj_turn(5, 1)
             adj_turn(5, 2)
-            stage2(4, 0)
+            finish(2, 1)
+            adj_quant(4)
             finish(3, 0)
+            stage2(4, 0)
             finish(3, 1)
             adj_quant(5)
-            finish(4, 0)
             stage2(4, 1)
+            finish(4, 0)
             finish(4, 1)
             stage2(5, 0)
-            finish(5, 0)
             stage2(5, 1)
+            finish(5, 0)
             finish(5, 1, 2)

from contextlib import ExitStack

import concourse.mybir as mybir
from concourse.masks import make_identity

NODES, FEAT, HID = 1536, 512, 512

F32 = mybir.dt.float32
BF16 = mybir.dt.bfloat16
I32 = mybir.dt.int32
U32 = mybir.dt.uint32
U8 = mybir.dt.uint8
E4M3 = mybir.dt.float8_e4m3fn
E4M3X4 = mybir.dt.float8_e4m3fn_x4
E2M1X4 = mybir.dt.float4_e2m1fn_x4
ALU = mybir.AluOpType
ACT = mybir.ActivationFunctionType

P = 128
K_PASS = 4 * P
PASSES = NODES // K_PASS
PAIR_ROWS = 2 * P
PAIRS = NODES // PAIR_ROWS

FLOPS = 2 * NODES * FEAT * HID + 2 * NODES * NODES * HID


def tile_gcn_pa_w4_kernel(tc, x_init, adj_bytes, adj_scale, w_words, w_scales, b1, out):
    nc = tc.nc
    with ExitStack() as ctx:
        keep = ctx.enter_context(tc.tile_pool(name="keep", bufs=1))
        a_in = ctx.enter_context(tc.tile_pool(name="a_in", bufs=PAIRS))
        x_in = ctx.enter_context(tc.tile_pool(name="x_in", bufs=PASSES))
        wide = ctx.enter_context(tc.tile_pool(name="wide", bufs=3))
        narrow = ctx.enter_context(tc.tile_pool(name="narrow", bufs=3))
        flipped = ctx.enter_context(tc.tile_pool(name="flipped", bufs=2))
        results = ctx.enter_context(tc.tile_pool(name="results", bufs=PAIRS))
        tp = ctx.enter_context(tc.psum_pool(name="tp", bufs=5))
        sums = ctx.enter_context(tc.psum_pool(name="sums", bufs=3))

        ident = keep.tile([P, P], F32, name="ident")
        scale_cols = [keep.tile([P, 4], F32, name="scale_cols%d" % g) for g in range(PASSES)]
        scale = keep.tile([P, NODES], F32, name="scale")
        bias = keep.tile([P, HID], BF16, name="bias")
        bias_rows = keep.tile([P, P], BF16, name="bias_rows")
        bias_rows_f32 = keep.tile([P, P], F32, name="bias_rows_f32")
        bias_col = keep.tile([P, 4], F32, name="bias_col")
        w_codes = keep.tile([P, 2 * HID], U8, name="w_codes", align_bytes=64)
        w_plane = keep.tile([P, HID], U8, name="w_plane", align_bytes=64)
        x_codes = keep.tile([P, PASSES, K_PASS], U32, name="x_codes", align_bytes=64)
        x_plane = keep.tile([P, PASSES, K_PASS], U8, name="x_plane", align_bytes=64)
        s_codes = keep.tile([P, PASSES, HID], U32, name="s_codes", align_bytes=64)
        s_plane = keep.tile([P, PASSES, HID], U8, name="s_plane", align_bytes=64)
        a_codes = keep.tile([P, PAIRS, PASSES, PAIR_ROWS], U32, name="a_codes", align_bytes=64)
        a_plane = keep.tile([P, PAIRS, PASSES, PAIR_ROWS], U8, name="a_plane", align_bytes=64)
        a_vals = keep.tile([P, PAIRS, 2, NODES], BF16, name="a_vals")

        a_raw, x_raw, x_grp, s_grp, a_grp = {}, {}, {}, {}, {}
        acc, flip, result = {}, {}, {}

        def load_scale(g):
            by_partition = adj_scale[:, K_PASS * g : K_PASS * (g + 1)].rearrange("o (p t) -> p (o t)", t=4)
            nc.sync.dma_start(out=scale_cols[g][:], in_=by_partition)

        def load_adj(q, first=0, last=NODES):
            if first == 0:
                raw = a_in.tile([P, 2, NODES], U8, name="raw")
                a_raw[q] = raw
            cols = slice(first, last)
            rows = adj_bytes[PAIR_ROWS * q : PAIR_ROWS * (q + 1), cols]
            nc.sync.dma_start(out=a_raw[q][:, :, cols], in_=rows.rearrange("(m j) k -> m j k", j=2))

        def load_x(g, c=0, pieces=1):
            if c == 0:
                x = x_in.tile([P, 4, FEAT], BF16, name="x")
                x_raw[g] = x
            ts = slice(4 // pieces * c, 4 // pieces * (c + 1))
            rows = x_init[K_PASS * g : K_PASS * (g + 1), :].rearrange("(m t) f -> m t f", t=4)
            nc.sync.dma_start(out=x_raw[g][:, ts, :], in_=rows[:, ts, :])

        def load_w_codes():
            nc.sync.dma_start(out=w_codes[:].bitcast(I32), in_=w_words[0].bitcast(I32))

        def load_w_plane():
            for quad in range(4):
                nc.sync.dma_start(
                    out=w_plane[32 * quad : 32 * quad + 4, :].bitcast(I32),
                    in_=w_scales[0, 4 * quad : 4 * quad + 4, :].bitcast(I32),
                )

        def spread_scale(g):
            bank = tp.tile([P, 4, P], F32, name="bank")
            for t in range(4):
                nc.tensor.transpose(bank[:, t, :], scale_cols[g][:, t : t + 1].to_broadcast([P, P]), ident[:])
            out_ap = scale[:, K_PASS * g : K_PASS * (g + 1)].rearrange("p (n t) -> p n t", t=4)
            in_ap = bank[:].rearrange("p t n -> p n t")
            if g == 0:
                nc.vector.tensor_copy(out=out_ap, in_=in_ap)
            else:
                nc.scalar.copy(out=out_ap, in_=in_ap)

        def turn_bias():
            nc.vector.tensor_copy(out=bias_rows_f32[:], in_=bias_rows[:])
            bank = tp.tile([P, 4, P], F32, name="bank")
            nc.tensor.transpose(bank[:, 0, :], bias_rows_f32[:], ident[:])
            nc.scalar.copy(out=bias_col[:], in_=bank[:, 0, 0:4])

        def adj_mult(i, c=0, pieces=1):
            q, j = divmod(i, 2)
            cols = slice(NODES // pieces * c, NODES // pieces * (c + 1))
            nc.vector.tensor_tensor(
                out=a_vals[:, q, j, cols],
                in0=a_raw[q][:, j, cols].bitcast(E4M3),
                in1=scale[:, cols],
                op=ALU.mult,
            )

        def turn(runs, grouped):
            bank = tp.tile([P, 4, P], F32, name="bank")
            for a in range(2):
                for u in range(2):
                    nc.tensor.transpose(bank[:, 2 * a + u, :], runs[a][:, u : 2 * P : 2], ident[:])
            nc.scalar.copy(
                out=grouped.bitcast(F32).rearrange("p (a m u) -> p a m u", a=2, u=2),
                in_=bank[:].rearrange("p (a u) m -> p a m u", a=2),
            )

        def x_turn(g, b):
            if b == 0:
                grouped = wide.tile([P, 4 * K_PASS], BF16, name="x_grouped", align_bytes=64)
                x_grp[g] = grouped
            runs = [x_raw[g][:, 2 * b + a, :].bitcast(F32) for a in range(2)]
            turn(runs, x_grp[g][:, 8 * P * b : 8 * P * (b + 1)])

        def x_quant(g):
            nc.vector.quantize_mx(out=x_codes[:, g, :].bitcast(E4M3X4), scales=x_plane[:, g, :], in_=x_grp[g][:])

        def stage1(g):
            grouped = wide.tile([P, 4 * HID], BF16, name="s_grouped", align_bytes=64)
            s_grp[g] = grouped
            for c in range(HID // P):
                bank = tp.tile([P, 4, P], F32, name="bank")
                for t in range(4):
                    cols = slice(P * t, P * (t + 1))
                    nc.tensor.matmul_mx(
                        out=bank[:, t, :],
                        lhsT=x_codes[:, g, cols].bitcast(E4M3X4),
                        lhsT_scale=x_plane[:, g, cols],
                        rhs=w_codes[:, 2 * P * c : 2 * P * (c + 1)].bitcast(E2M1X4),
                        rhs_scale=w_plane[:, P * c : P * (c + 1)],
                        start=True,
                        stop=True,
                    )
                nc.scalar.copy(
                    out=grouped[:, 4 * P * c : 4 * P * (c + 1)].rearrange("p (n t) -> p n t", t=4),
                    in_=bank[:].rearrange("p t n -> p n t"),
                )

        def s_quant(g):
            nc.vector.quantize_mx(out=s_codes[:, g, :].bitcast(E4M3X4), scales=s_plane[:, g, :], in_=s_grp[g][:])

        def adj_turn(q, g):
            if g == 0:
                grouped = narrow.tile([P, PASSES, 4 * PAIR_ROWS], BF16, name="a_grouped", align_bytes=64)
                a_grp[q] = grouped
            runs = [a_vals[:, q, j, K_PASS * g : K_PASS * (g + 1)].bitcast(F32) for j in range(2)]
            turn(runs, a_grp[q][:, g, :])

        def adj_quant(q):
            for gs in (slice(0, 2), slice(2, 3)):
                nc.vector.quantize_mx(
                    out=a_codes[:, q, gs, :].rearrange("p g r -> p (g r)").bitcast(E4M3X4),
                    scales=a_plane[:, q, gs, :].rearrange("p g r -> p (g r)"),
                    in_=a_grp[q][:, gs, :].rearrange("p g r -> p (g r)"),
                )

        def out_rows(q):
            return out[PAIR_ROWS * q : PAIR_ROWS * (q + 1), :].rearrange("(m j) h -> m j h", j=2)

        def stage2(q, j):
            total = sums.tile([P, HID], F32, name="total")
            acc[q, j] = total
            for g in range(PASSES):
                cols = slice(P * j, P * (j + 1))
                nc.tensor.matmul_mx(
                    out=total[:],
                    lhsT=a_codes[:, q, g, cols].bitcast(E4M3X4),
                    lhsT_scale=a_plane[:, q, g, cols],
                    rhs=s_codes[:, g, :].bitcast(E4M3X4),
                    rhs_scale=s_plane[:, g, :],
                    start=(g == 0),
                    stop=(g == PASSES - 1),
                )

        def finish(q, j, pieces=1):
            if j == 0:
                res = results.tile([P, 2, HID], F32, name="res")
                result[q] = res
            for c in range(pieces):
                cols = slice(HID // pieces * c, HID // pieces * (c + 1))
                part = result[q][:, j, cols]
                nc.vector.tensor_tensor(out=part, in0=acc[q, j][:, cols], in1=bias[:, cols], op=ALU.add)
                nc.scalar.activation(out=part, in_=part, func=ACT.Relu)
                nc.sync.dma_start(out=out_rows(q)[:, j, cols], in_=part)

        def stage2_flipped(q, h):
            if h == 0:
                flat = flipped.tile([P, 4, PAIR_ROWS], F32, name="flat")
                flip[q] = flat
            total = sums.tile([P, HID], F32, name="total")
            halves = [total[:, PAIR_ROWS * i : PAIR_ROWS * (i + 1)] for i in range(2)]
            for i in range(2):
                cols = slice(P * (2 * h + i), P * (2 * h + i + 1))
                for g in range(PASSES):
                    nc.tensor.matmul_mx(
                        out=halves[i],
                        lhsT=s_codes[:, g, cols].bitcast(E4M3X4),
                        lhsT_scale=s_plane[:, g, cols],
                        rhs=a_codes[:, q, g, :].bitcast(E4M3X4),
                        rhs_scale=a_plane[:, q, g, :],
                        start=(g == 0),
                        stop=(g == PASSES - 1),
                    )
            for i in range(2):
                c = 2 * h + i
                nc.scalar.activation(
                    out=flip[q][:, c, :], in_=halves[i], func=ACT.Relu, bias=bias_col[:, c : c + 1]
                )

        def flip_back(q, j):
            if j == 0:
                res = results.tile([P, 2, HID], F32, name="res")
                result[q] = res
            bank = tp.tile([P, 4, P], F32, name="bank")
            for c in range(4):
                nc.tensor.transpose(bank[:, c, :], flip[q][:, c, P * j : P * (j + 1)], ident[:])
            nc.scalar.copy(out=result[q][:, j, :], in_=bank[:].rearrange("p c m -> p (c m)"))
            nc.sync.dma_start(out=out_rows(q)[:, j, :], in_=result[q][:, j, :])

        with tc.manual_schedule():
            make_identity(nc, ident[:])
            nc.gpsimd.memset(w_plane[:].bitcast(I32), 0)
            nc.gpsimd.memset(bias_rows[:], 0.0)
            load_scale(0)
            load_adj(0, 0, K_PASS)
            load_scale(1)
            load_scale(2)
            load_x(0, 0, 2)
            load_adj(0, K_PASS, NODES)
            load_x(0, 1, 2)
            load_x(1)
            load_adj(1)
            load_x(2)
            load_w_codes()
            load_w_plane()
            nc.sync.dma_start(out=bias_rows[0:4, :], in_=b1.rearrange("(c m) -> c m", m=P))
            for q in range(2, PAIRS):
                load_adj(q)
            nc.sync.dma_start(out=bias[:], in_=b1.partition_broadcast(P))

            spread_scale(0)
            spread_scale(1)
            spread_scale(2)
            adj_mult(0, 0, 3)
            adj_mult(1, 0, 3)
            x_turn(0, 0)
            x_turn(0, 1)
            adj_mult(0, 1, 3)
            adj_mult(1, 1, 3)
            adj_turn(0, 0)
            x_turn(1, 0)
            x_turn(1, 1)
            adj_mult(0, 2, 3)
            adj_mult(1, 2, 3)
            adj_turn(0, 1)
            x_quant(0)
            x_turn(2, 0)
            x_turn(2, 1)
            adj_mult(2)
            x_quant(1)
            adj_turn(0, 2)
            x_quant(2)
            stage1(0)
            adj_mult(3)
            stage1(1)
            adj_mult(4)
            stage1(2)
            turn_bias()
            adj_mult(5)
            adj_quant(0)
            adj_turn(1, 0)
            adj_turn(1, 1)
            adj_turn(1, 2)
            adj_turn(2, 0)
            adj_turn(2, 1)
            adj_turn(2, 2)
            s_quant(0)
            s_quant(1)
            s_quant(2)
            adj_mult(6)
            adj_quant(1)
            adj_quant(2)
            adj_mult(7)
            stage2_flipped(0, 0)
            stage2_flipped(0, 1)
            stage2_flipped(1, 0)
            stage2_flipped(1, 1)
            stage2(2, 0)
            flip_back(0, 0)
            adj_turn(3, 0)
            adj_turn(3, 1)
            adj_turn(3, 2)
            flip_back(1, 0)
            adj_mult(8)
            adj_mult(9)
            adj_quant(3)
            stage2(2, 1)
            finish(2, 0)
            adj_mult(10)
            flip_back(0, 1)
            adj_turn(4, 0)
            adj_turn(4, 1)
            adj_turn(4, 2)
            stage2(3, 0)
            stage2(3, 1)
            adj_mult(11)
            flip_back(1, 1)
            adj_turn(5, 0)
            adj_turn(5, 1)
            adj_turn(5, 2)
            finish(2, 1)
            adj_quant(4)
            finish(3, 0)
            stage2(4, 0)
            finish(3, 1)
            adj_quant(5)
            stage2(4, 1)
            finish(4, 0)
            finish(4, 1)
            stage2(5, 0)
            stage2(5, 1)
            finish(5, 0)
            finish(5, 1, 2)
